import numpy as np
import ml_dtypes

BF16 = ml_dtypes.bfloat16


def bf(x):
    return np.asarray(x, np.float32).astype(BF16)


def f32(x):
    return np.asarray(x, np.float32)


def f64(x):
    return np.asarray(x).astype(np.float64)


def striped(idx):
    return np.tile(idx.reshape(-1, 16).T, (8, 1))


D, C, S, B, M, T, N = 128, 256, 2048, 16, 128, 4, 8192
SCALE = 0.6


def setup_inputs():
    return {"table": f32(SCALE * np.random.standard_normal((C, S))), "offs": striped(np.concatenate([np.random.permutation(S) for _ in range(T)]))}


def reference(table, offs):
    idx = offs[:16].T.reshape(-1)
    e = f64(table)[:, idx].reshape(C, T, B, M).sum(axis=1)
    a, v = e[:D], e[D:]
    u1 = a.sum(axis=2) / M
    z = (a * u1[:, :, None]).sum(axis=0)
    w = np.exp(z - z.max(axis=1, keepdims=True))
    p = w / w.sum(axis=1, keepdims=True)
    return u1 + (v * p[None, :, :]).sum(axis=2)

@@ -1,0 +1,147 @@
+import concourse.mybir as mybir
+from concourse.masks import make_identity
+
+F32 = mybir.dt.float32
+BF16 = mybir.dt.bfloat16
+U16 = mybir.dt.uint16
+ADD = mybir.AluOpType.add
+MULT = mybir.AluOpType.mult
+COPY = mybir.ActivationFunctionType.Copy
+EXP = mybir.ActivationFunctionType.Exp
+X = mybir.AxisListType.X
+
+P = 128
+VOCAB = 2048
+STORIES = 16
+SENTENCES = 128
+WORDS = 4
+COLS = STORIES * SENTENCES
+HALF = COLS // 2
+BANK = 512
+
+FLOPS = 2 * 2 * P * COLS
+
+
+def tile_encodermemnn_kernel(tc, table, offs, out):
+    nc = tc.nc
+    with (
+        tc.tile_pool(name="held", bufs=1) as held,
+        tc.tile_pool(name="a_passes", bufs=3) as a_passes,
+        tc.tile_pool(name="pieces", bufs=2) as pieces,
+        tc.psum_pool(name="psum", bufs=1) as psum,
+    ):
+        offsets = held.tile([P, WORDS * COLS // 16], U16, name="offsets")
+        nc.sync.dma_start(offsets[:], offs)
+        address_table = held.tile([P, VOCAB], F32, name="address_table")
+        nc.sync.dma_start(address_table[:], table[0:P, :])
+
+        ones = held.tile([P, P], BF16, name="ones")
+        nc.gpsimd.memset(ones[:], 1.0)
+        selector = held.tile([P, 2 * STORIES - 1], BF16, name="selector")
+        nc.gpsimd.memset(selector[:], 0.0)
+        nc.gpsimd.memset(selector[:, STORIES - 1 : STORIES], 1.0)
+        story_ones = held.tile([STORIES, P], F32, name="story_ones")
+        nc.gpsimd.memset(story_ones[:], 1.0)
+        story_identity = held.tile([STORIES, STORIES], F32, name="story_identity")
+        make_identity(nc, story_identity[:])
+
+        warm = held.tile([P, 1], F32, name="warm", tag="value_table")
+        nc.gpsimd.memset(warm[:], 0.0)
+        nc.scalar.activation(warm[:], warm[:], EXP)
+        value_table = held.tile([P, VOCAB], F32, name="value_table", tag="value_table")
+        nc.sync.dma_start(value_table[:], table[P : 2 * P, :])
+
+        def late_tile(turn, dtype):
+            return held.tile([P, COLS], dtype, name=f"late{turn}", tag=f"slot{turn % 3}")
+
+        def story(b):
+            return slice(b * SENTENCES, (b + 1) * SENTENCES)
+
+        def add_words(window, t, first, shorter, longer):
+            entry = t * COLS + first
+            words = window[:].indirect(offsets[:, entry // 16 : (entry + longer.shape[1]) // 16])
+            if t == 0:
+                nc.vector.tensor_copy(longer, words)
+            else:
+                nc.vector.tensor_tensor(longer, words, shorter, ADD)
+
+        def pass_by_halves(window, t, sums, longer):
+            for first in range(0, COLS, HALF):
+                half = slice(first, first + HALF)
+                add_words(window, t, first, None if t == 0 else sums[:, half], longer[:, half])
+
+        a = None
+        for t in range(WORDS):
+            longer = a_passes.tile([P, COLS], F32, name="a")
+            pass_by_halves(address_table, t, a, longer)
+            a = longer
+
+        u1 = held.tile([P, STORIES], F32, name="u1")
+        unused = held.tile([P, SENTENCES], F32, name="unused")
+        products = late_tile(0, BF16)
+        for b in range(STORIES):
+            nc.scalar.activation(
+                unused[:], a[:, story(b)], COPY, scale=1.0 / SENTENCES, accum_out=u1[:, b : b + 1]
+            )
+            nc.scalar.activation(products[:, story(b)], a[:, story(b)], COPY, scale=u1[:, b : b + 1])
+
+        z_by_story = psum.tile([STORIES, SENTENCES], F32, name="z_by_story")
+        for b in range(STORIES):
+            nc.tensor.matmul(
+                z_by_story[:],
+                selector[:, STORIES - 1 - b : 2 * STORIES - 1 - b],
+                products[:, story(b)],
+                start=(b == 0),
+                stop=(b == STORIES - 1),
+            )
+        z = psum.tile([P, COLS], F32, name="z")
+        for first in range(0, COLS, BANK):
+            bank = slice(first, first + BANK)
+            nc.tensor.matmul(z[:, bank], ones[:], products[:, bank], start=True, stop=True)
+
+        minus_max = held.tile([STORIES, 1], F32, name="minus_max")
+        nc.vector.reduce_max(minus_max[:], z_by_story[:], axis=X, negate=True)
+        diagonal = held.tile([STORIES, STORIES], F32, name="diagonal")
+        nc.scalar.activation(diagonal[:], story_identity[:], COPY, scale=minus_max[:, 0:1])
+        shift_psum = psum.tile([P, STORIES], F32, name="shift_psum")
+        nc.tensor.matmul(shift_psum[:], story_ones[:], diagonal[:], start=True, stop=True)
+        shift = held.tile([P, STORIES], F32, name="shift")
+        nc.scalar.copy(shift[:], shift_psum[:])
+
+        w = held.tile([P, COLS], F32, name="w")
+        w_sum = held.tile([P, STORIES], F32, name="w_sum")
+        for b in range(STORIES):
+            nc.scalar.activation(
+                w[:, story(b)], z[:, story(b)], EXP, bias=shift[:, b : b + 1], accum_out=w_sum[:, b : b + 1]
+            )
+        w_scale = held.tile([P, STORIES], F32, name="w_scale")
+        nc.vector.reciprocal(w_scale[:], w_sum[:])
+
+        v = None
+        for t in range(WORDS - 1):
+            longer = late_tile(1 + t, F32)
+            pass_by_halves(value_table, t, v, longer)
+            v = longer
+
+        weighted = held.tile([P, COLS], F32, name="weighted")
+        hop2 = held.tile([P, STORIES, 2], F32, name="hop2")
+        for first in range(0, COLS, BANK):
+            piece = slice(first, first + BANK)
+            v_piece = pieces.tile([P, BANK], F32, name="v_piece")
+            add_words(value_table, WORDS - 1, first, v[:, piece], v_piece[:])
+            nc.vector.tensor_tensor(weighted[:, piece], v_piece[:], w[:, piece], MULT)
+            stories = range(first // SENTENCES, (first + BANK) // SENTENCES)
+            if first + BANK < COLS:
+                for b in stories:
+                    nc.scalar.activation(unused[:], weighted[:, story(b)], COPY, accum_out=hop2[:, b, 0:1])
+            else:
+                nc.vector.reduce_sum(
+                    hop2[:, stories[0] : STORIES, 0],
+                    weighted[:, piece].rearrange("p (b m) -> p b m", m=SENTENCES),
+                    axis=X,
+                )
+
+        result = held.tile([P, STORIES], F32, name="result")
+        nc.vector.tensor_tensor(result[:], hop2[:, :, 0], w_scale[:], MULT)
+        nc.vector.tensor_tensor(result[:], result[:], u1[:], ADD)
+        nc.sync.dma_start(out, result[:])

@@ -7,7 +7,9 @@ U16 = mybir.dt.uint16
 ADD = mybir.AluOpType.add
 MULT = mybir.AluOpType.mult
 COPY = mybir.ActivationFunctionType.Copy
+IDENTITY = mybir.ActivationFunctionType.Identity
 EXP = mybir.ActivationFunctionType.Exp
+LN = mybir.ActivationFunctionType.Ln
 X = mybir.AxisListType.X
 
 P = 128
@@ -17,7 +19,9 @@ SENTENCES = 128
 WORDS = 4
 COLS = STORIES * SENTENCES
 HALF = COLS // 2
+HALF_STORIES = STORIES // 2
 BANK = 512
+BANK_STORIES = BANK // SENTENCES
 
 FLOPS = 2 * 2 * P * COLS
 
@@ -27,7 +31,6 @@ def tile_encodermemnn_kernel(tc, table, offs, out):
     with (
         tc.tile_pool(name="held", bufs=1) as held,
         tc.tile_pool(name="a_passes", bufs=3) as a_passes,
-        tc.tile_pool(name="pieces", bufs=2) as pieces,
         tc.psum_pool(name="psum", bufs=1) as psum,
     ):
         offsets = held.tile([P, WORDS * COLS // 16], U16, name="offsets")
@@ -35,24 +38,22 @@ def tile_encodermemnn_kernel(tc, table, offs, out):
         address_table = held.tile([P, VOCAB], F32, name="address_table")
         nc.sync.dma_start(address_table[:], table[0:P, :])
 
-        ones = held.tile([P, P], BF16, name="ones")
-        nc.gpsimd.memset(ones[:], 1.0)
+        identity = held.tile([P, P], F32, name="identity")
+        make_identity(nc, identity[:])
+        story_identity = identity[0:STORIES, 0:STORIES]
         selector = held.tile([P, 2 * STORIES - 1], BF16, name="selector")
         nc.gpsimd.memset(selector[:], 0.0)
         nc.gpsimd.memset(selector[:, STORIES - 1 : STORIES], 1.0)
+        ones = held.tile([P, P], BF16, name="ones")
+        nc.gpsimd.memset(ones[:], 1.0)
         story_ones = held.tile([STORIES, P], F32, name="story_ones")
         nc.gpsimd.memset(story_ones[:], 1.0)
-        story_identity = held.tile([STORIES, STORIES], F32, name="story_identity")
-        make_identity(nc, story_identity[:])
 
         warm = held.tile([P, 1], F32, name="warm", tag="value_table")
-        nc.gpsimd.memset(warm[:], 0.0)
-        nc.scalar.activation(warm[:], warm[:], EXP)
+        nc.gpsimd.memset(warm[:], 1.0)
+        nc.scalar.activation(warm[:], warm[:], LN)
         value_table = held.tile([P, VOCAB], F32, name="value_table", tag="value_table")
         nc.sync.dma_start(value_table[:], table[P : 2 * P, :])
-
-        def late_tile(turn, dtype):
-            return held.tile([P, COLS], dtype, name=f"late{turn}", tag=f"slot{turn % 3}")
 
         def story(b):
             return slice(b * SENTENCES, (b + 1) * SENTENCES)
@@ -65,83 +66,133 @@ def tile_encodermemnn_kernel(tc, table, offs, out):
             else:
                 nc.vector.tensor_tensor(longer, words, shorter, ADD)
 
-        def pass_by_halves(window, t, sums, longer):
-            for first in range(0, COLS, HALF):
-                half = slice(first, first + HALF)
-                add_words(window, t, first, None if t == 0 else sums[:, half], longer[:, half])
-
         a = None
         for t in range(WORDS):
             longer = a_passes.tile([P, COLS], F32, name="a")
-            pass_by_halves(address_table, t, a, longer)
+            for first in (0, HALF):
+                half = slice(first, first + HALF)
+                add_words(address_table, t, first, None if t == 0 else a[:, half], longer[:, half])
             a = longer
 
         u1 = held.tile([P, STORIES], F32, name="u1")
         unused = held.tile([P, SENTENCES], F32, name="unused")
-        products = late_tile(0, BF16)
-        for b in range(STORIES):
-            nc.scalar.activation(
-                unused[:], a[:, story(b)], COPY, scale=1.0 / SENTENCES, accum_out=u1[:, b : b + 1]
-            )
-            nc.scalar.activation(products[:, story(b)], a[:, story(b)], COPY, scale=u1[:, b : b + 1])
-
-        z_by_story = psum.tile([STORIES, SENTENCES], F32, name="z_by_story")
+        products = held.tile([P, COLS], BF16, name="products")
+        for first in (0, HALF_STORIES):
+            for b in range(first, first + HALF_STORIES):
+                nc.scalar.activation(
+                    unused[:], a[:, story(b)], COPY, scale=1.0 / SENTENCES, accum_out=u1[:, b : b + 1]
+                )
+            for b in range(first, first + HALF_STORIES):
+                nc.scalar.activation(products[:, story(b)], a[:, story(b)], COPY, scale=u1[:, b : b + 1])
+        z = psum.tile([STORIES, SENTENCES], F32, name="z")
         for b in range(STORIES):
             nc.tensor.matmul(
-                z_by_story[:],
+                z[:],
                 selector[:, STORIES - 1 - b : 2 * STORIES - 1 - b],
                 products[:, story(b)],
                 start=(b == 0),
                 stop=(b == STORIES - 1),
             )
-        z = psum.tile([P, COLS], F32, name="z")
-        for first in range(0, COLS, BANK):
-            bank = slice(first, first + BANK)
-            nc.tensor.matmul(z[:, bank], ones[:], products[:, bank], start=True, stop=True)
 
+        z_spread = []
+        for first in range(HALF, COLS, BANK):
+            bank = psum.tile([P, BANK], F32, name=f"z_spread{first}")
+            nc.tensor.matmul(bank[:], ones[:], products[:, first : first + BANK], start=True, stop=True)
+            z_spread.append(bank)
+
+        def v_tile(name, tag):
+            return held.tile([P, HALF], F32, name=name, tag=tag)
+
+        banks = (slice(0, BANK), slice(BANK, HALF))
+        first0 = v_tile("first0", "first0")
+        add_words(value_table, 0, 0, None, first0[:])
+        last0 = v_tile("last0", "last0")
+        add_words(value_table, 0, HALF, None, last0[:])
+        first1 = v_tile("first1", "first1")
+        add_words(value_table, 1, 0, first0[:], first1[:])
+        last1 = v_tile("last1", "last1")
+        add_words(value_table, 1, HALF, last0[:], last1[:])
+
+        z_copy = held.tile([STORIES, SENTENCES], F32, name="z_copy", tag="after_maximum")
+        nc.scalar.copy(z_copy[:], z[:])
         minus_max = held.tile([STORIES, 1], F32, name="minus_max")
-        nc.vector.reduce_max(minus_max[:], z_by_story[:], axis=X, negate=True)
+        nc.vector.reduce_max(minus_max[:], z_copy[:], axis=X, negate=True)
+        w = held.tile([STORIES, SENTENCES], F32, name="w")
+        w_sum = held.tile([STORIES, 1], F32, name="w_sum")
+        nc.scalar.activation(w[:], z[:], EXP, bias=minus_max[:, 0:1], accum_out=w_sum[:])
+        log_sum = held.tile([STORIES, 1], F32, name="log_sum")
+        nc.scalar.activation(log_sum[:], w_sum[:], LN)
+        shift = held.tile([STORIES, 1], F32, name="shift")
+        nc.scalar.activation(shift[:], log_sum[:], IDENTITY, scale=-1.0, bias=minus_max[:, 0:1])
+        p = held.tile([STORIES, SENTENCES], F32, name="p")
+        nc.scalar.activation(p[:], z[:], EXP, bias=shift[:, 0:1])
+
         diagonal = held.tile([STORIES, STORIES], F32, name="diagonal")
-        nc.scalar.activation(diagonal[:], story_identity[:], COPY, scale=minus_max[:, 0:1])
-        shift_psum = psum.tile([P, STORIES], F32, name="shift_psum")
-        nc.tensor.matmul(shift_psum[:], story_ones[:], diagonal[:], start=True, stop=True)
-        shift = held.tile([P, STORIES], F32, name="shift")
-        nc.scalar.copy(shift[:], shift_psum[:])
-
-        w = held.tile([P, COLS], F32, name="w")
-        w_sum = held.tile([P, STORIES], F32, name="w_sum")
-        for b in range(STORIES):
+        nc.scalar.activation(diagonal[:], story_identity, COPY, scale=shift[:, 0:1])
+        small_psum = psum.tile([P, 2 * STORIES], F32, name="small_psum")
+        shift_psum = small_psum[:, 0:STORIES]
+        p_turned_psum = small_psum[:, STORIES : 2 * STORIES]
+        nc.tensor.matmul(shift_psum, story_ones[:], diagonal[:], start=True, stop=True)
+        nc.tensor.matmul(p_turned_psum, p[:], story_identity, start=True, stop=True)
+        small = held.tile([P, 2 * STORIES], F32, name="small")
+        nc.scalar.copy(small[:], small_psum[:])
+        shift_spread = small[:, 0:STORIES]
+        p_turned = small[:, STORIES : 2 * STORIES]
+        p_spread = held.tile([P, HALF], F32, name="p_spread")
+        for k in range(HALF_STORIES):
+            b = HALF_STORIES + k
             nc.scalar.activation(
-                w[:, story(b)], z[:, story(b)], EXP, bias=shift[:, b : b + 1], accum_out=w_sum[:, b : b + 1]
+                p_spread[:, story(k)],
+                z_spread[k // BANK_STORIES][:, story(k % BANK_STORIES)],
+                EXP,
+                bias=shift_spread[:, b : b + 1],
             )
-        w_scale = held.tile([P, STORIES], F32, name="w_scale")
-        nc.vector.reciprocal(w_scale[:], w_sum[:])
+        u1_share = held.tile([P, STORIES], F32, name="u1_share")
+        nc.scalar.activation(u1_share[:], u1[:], COPY, scale=1.0 / SENTENCES)
 
-        v = None
-        for t in range(WORDS - 1):
-            longer = late_tile(1 + t, F32)
-            pass_by_halves(value_table, t, v, longer)
-            v = longer
-
-        weighted = held.tile([P, COLS], F32, name="weighted")
-        hop2 = held.tile([P, STORIES, 2], F32, name="hop2")
-        for first in range(0, COLS, BANK):
-            piece = slice(first, first + BANK)
-            v_piece = pieces.tile([P, BANK], F32, name="v_piece")
-            add_words(value_table, WORDS - 1, first, v[:, piece], v_piece[:])
-            nc.vector.tensor_tensor(weighted[:, piece], v_piece[:], w[:, piece], MULT)
-            stories = range(first // SENTENCES, (first + BANK) // SENTENCES)
-            if first + BANK < COLS:
-                for b in stories:
-                    nc.scalar.activation(unused[:], weighted[:, story(b)], COPY, accum_out=hop2[:, b, 0:1])
-            else:
-                nc.vector.reduce_sum(
-                    hop2[:, stories[0] : STORIES, 0],
-                    weighted[:, piece].rearrange("p (b m) -> p b m", m=SENTENCES),
-                    axis=X,
-                )
+        first2 = v_tile("first2", "after_maximum")
+        for bank in banks:
+            add_words(value_table, 2, bank.start, first1[:, bank], first2[:, bank])
+        first3 = v_tile("first3", "first3")
+        for bank in banks:
+            add_words(value_table, 3, bank.start, first2[:, bank], first3[:, bank])
+        last2 = v_tile("last2", "after_maximum")
+        for bank in banks:
+            add_words(value_table, 2, HALF + bank.start, last1[:, bank], last2[:, bank])
+        last3 = v_tile("last3", "last3")
+        for bank in banks:
+            add_words(value_table, 3, HALF + bank.start, last2[:, bank], last3[:, bank])
 
         result = held.tile([P, STORIES], F32, name="result")
-        nc.vector.tensor_tensor(result[:], hop2[:, :, 0], w_scale[:], MULT)
-        nc.vector.tensor_tensor(result[:], result[:], u1[:], ADD)
+        v_turned = held.tile([P, HALF], F32, name="v_turned")
+        for bank in banks:
+            turned = psum.tile([P, BANK], F32, name=f"turned{bank.start}")
+            for k in range(BANK_STORIES):
+                b = bank.start // SENTENCES + k
+                nc.tensor.transpose(turned[:, story(k)], first3[:, story(b)], identity[:])
+            nc.scalar.copy(v_turned[:, bank], turned[:])
+        hop2 = psum.tile([P, HALF_STORIES], F32, name="hop2")
+        for b in range(HALF_STORIES):
+            nc.tensor.matmul(hop2[:, b : b + 1], v_turned[:, story(b)], p_turned[:, b : b + 1], start=True, stop=True)
+
+        weighted = held.tile([P, BANK], F32, name="weighted")
+        nc.vector.tensor_tensor(weighted[:], last3[:, 0:BANK], p_spread[:, 0:BANK], MULT)
+        for k in range(BANK_STORIES):
+            b = HALF_STORIES + k
+            nc.scalar.activation(
+                unused[:], weighted[:, story(k)], IDENTITY, bias=u1_share[:, b : b + 1], accum_out=result[:, b : b + 1]
+            )
+        unused_product = held.tile([P, SENTENCES], F32, name="unused_product")
+        for k in range(BANK_STORIES, HALF_STORIES):
+            b = HALF_STORIES + k
+            nc.vector.scalar_tensor_tensor(
+                unused_product[:],
+                last3[:, story(k)],
+                u1[:, b : b + 1],
+                p_spread[:, story(k)],
+                ADD,
+                MULT,
+                accum_out=result[:, b : b + 1],
+            )
+        nc.vector.tensor_tensor(result[:, 0:HALF_STORIES], hop2[:], u1[:, 0:HALF_STORIES], ADD)
         nc.sync.dma_start(out, result[:])

@@ -9,7 +9,6 @@ MULT = mybir.AluOpType.mult
 COPY = mybir.ActivationFunctionType.Copy
 IDENTITY = mybir.ActivationFunctionType.Identity
 EXP = mybir.ActivationFunctionType.Exp
-LN = mybir.ActivationFunctionType.Ln
 X = mybir.AxisListType.X
 
 P = 128
@@ -32,6 +31,7 @@ def tile_encodermemnn_kernel(tc, table, offs, out):
         tc.tile_pool(name="held", bufs=1) as held,
         tc.tile_pool(name="a_passes", bufs=3) as a_passes,
         tc.psum_pool(name="psum", bufs=1) as psum,
+        tc.psum_pool(name="small_psum", bufs=1) as small_psum,
     ):
         offsets = held.tile([P, WORDS * COLS // 16], U16, name="offsets")
         nc.sync.dma_start(offsets[:], offs)
@@ -50,8 +50,8 @@ def tile_encodermemnn_kernel(tc, table, offs, out):
         nc.gpsimd.memset(story_ones[:], 1.0)
 
         warm = held.tile([P, 1], F32, name="warm", tag="value_table")
-        nc.gpsimd.memset(warm[:], 1.0)
-        nc.scalar.activation(warm[:], warm[:], LN)
+        nc.gpsimd.memset(warm[:], 0.0)
+        nc.scalar.activation(warm[:], warm[:], EXP)
         value_table = held.tile([P, VOCAB], F32, name="value_table", tag="value_table")
         nc.sync.dma_start(value_table[:], table[P : 2 * P, :])
 
@@ -100,68 +100,66 @@ def tile_encodermemnn_kernel(tc, table, offs, out):
             nc.tensor.matmul(bank[:], ones[:], products[:, first : first + BANK], start=True, stop=True)
             z_spread.append(bank)
 
-        def v_tile(name, tag):
-            return held.tile([P, HALF], F32, name=name, tag=tag)
-
         banks = (slice(0, BANK), slice(BANK, HALF))
-        first0 = v_tile("first0", "first0")
-        add_words(value_table, 0, 0, None, first0[:])
-        last0 = v_tile("last0", "last0")
-        add_words(value_table, 0, HALF, None, last0[:])
-        first1 = v_tile("first1", "first1")
-        add_words(value_table, 1, 0, first0[:], first1[:])
-        last1 = v_tile("last1", "last1")
-        add_words(value_table, 1, HALF, last0[:], last1[:])
+
+        def v_pass(t, first, shorter, name, tag):
+            longer = held.tile([P, HALF], F32, name=name, tag=tag)
+            for bank in banks:
+                add_words(value_table, t, first + bank.start, None if t == 0 else shorter[:, bank], longer[:, bank])
+            return longer
+
+        first0 = v_pass(0, 0, None, "first0", "first0")
+        first1 = v_pass(1, 0, first0, "first1", "first1")
+        first2 = v_pass(2, 0, first1, "first2", "first2")
+        first3 = v_pass(3, 0, first2, "first3", "first3")
+        last0 = v_pass(0, HALF, None, "last0", "first2")
 
         z_copy = held.tile([STORIES, SENTENCES], F32, name="z_copy", tag="after_maximum")
         nc.scalar.copy(z_copy[:], z[:])
         minus_max = held.tile([STORIES, 1], F32, name="minus_max")
         nc.vector.reduce_max(minus_max[:], z_copy[:], axis=X, negate=True)
         w = held.tile([STORIES, SENTENCES], F32, name="w")
-        w_sum = held.tile([STORIES, 1], F32, name="w_sum")
+        w_sum = held.tile([STORIES, 1], F32, name="w_sum", tag="after_reciprocal")
         nc.scalar.activation(w[:], z[:], EXP, bias=minus_max[:, 0:1], accum_out=w_sum[:])
-        log_sum = held.tile([STORIES, 1], F32, name="log_sum")
-        nc.scalar.activation(log_sum[:], w_sum[:], LN)
-        shift = held.tile([STORIES, 1], F32, name="shift")
-        nc.scalar.activation(shift[:], log_sum[:], IDENTITY, scale=-1.0, bias=minus_max[:, 0:1])
-        p = held.tile([STORIES, SENTENCES], F32, name="p")
-        nc.scalar.activation(p[:], z[:], EXP, bias=shift[:, 0:1])
 
-        diagonal = held.tile([STORIES, STORIES], F32, name="diagonal")
-        nc.scalar.activation(diagonal[:], story_identity, COPY, scale=shift[:, 0:1])
-        small_psum = psum.tile([P, 2 * STORIES], F32, name="small_psum")
-        shift_psum = small_psum[:, 0:STORIES]
-        p_turned_psum = small_psum[:, STORIES : 2 * STORIES]
-        nc.tensor.matmul(shift_psum, story_ones[:], diagonal[:], start=True, stop=True)
-        nc.tensor.matmul(p_turned_psum, p[:], story_identity, start=True, stop=True)
-        small = held.tile([P, 2 * STORIES], F32, name="small")
-        nc.scalar.copy(small[:], small_psum[:])
-        shift_spread = small[:, 0:STORIES]
-        p_turned = small[:, STORIES : 2 * STORIES]
-        p_spread = held.tile([P, HALF], F32, name="p_spread")
+        w_turned_psum = small_psum.tile([P, STORIES], F32, name="small_psum")
+        nc.tensor.matmul(w_turned_psum[:], w[:], story_identity, start=True, stop=True)
+        w_turned = held.tile([P, STORIES], F32, name="w_turned")
+        nc.scalar.copy(w_turned[:], w_turned_psum[:])
+
+        def spread(value, name):
+            diagonal = held.tile([STORIES, STORIES], F32, name=f"{name}_diagonal")
+            nc.scalar.activation(diagonal[:], story_identity, COPY, scale=value[:, 0:1])
+            on_psum = small_psum.tile([P, STORIES], F32, name="small_psum")
+            nc.tensor.matmul(on_psum[:], story_ones[:], diagonal[:], start=True, stop=True)
+            spread_value = held.tile([P, STORIES], F32, name=name)
+            nc.scalar.copy(spread_value[:], on_psum[:])
+            return spread_value
+
+        shift = spread(minus_max, "shift")
+        w_spread = held.tile([P, HALF], F32, name="w_spread")
         for k in range(HALF_STORIES):
             b = HALF_STORIES + k
             nc.scalar.activation(
-                p_spread[:, story(k)],
-                z_spread[k // BANK_STORIES][:, story(k % BANK_STORIES)],
-                EXP,
-                bias=shift_spread[:, b : b + 1],
+                w_spread[:, story(k)], z_spread[k // BANK_STORIES][:, story(k % BANK_STORIES)], EXP, bias=shift[:, b : b + 1]
+            )
+
+        last1 = v_pass(1, HALF, last0, "last1", "after_maximum")
+
+        w_scale = held.tile([STORIES, 1], F32, name="w_scale")
+        nc.vector.reciprocal(w_scale[:], w_sum[:])
+        scale_spread = spread(w_scale, "scale_spread")
+        p_last = held.tile([P, BANK], F32, name="p_last")
+        for k in range(BANK_STORIES):
+            b = STORIES - BANK_STORIES + k
+            nc.scalar.activation(
+                p_last[:, story(k)], w_spread[:, story(BANK_STORIES + k)], COPY, scale=scale_spread[:, b : b + 1]
             )
         u1_share = held.tile([P, STORIES], F32, name="u1_share")
         nc.scalar.activation(u1_share[:], u1[:], COPY, scale=1.0 / SENTENCES)
 
-        first2 = v_tile("first2", "after_maximum")
-        for bank in banks:
-            add_words(value_table, 2, bank.start, first1[:, bank], first2[:, bank])
-        first3 = v_tile("first3", "first3")
-        for bank in banks:
-            add_words(value_table, 3, bank.start, first2[:, bank], first3[:, bank])
-        last2 = v_tile("last2", "after_maximum")
-        for bank in banks:
-            add_words(value_table, 2, HALF + bank.start, last1[:, bank], last2[:, bank])
-        last3 = v_tile("last3", "last3")
-        for bank in banks:
-            add_words(value_table, 3, HALF + bank.start, last2[:, bank], last3[:, bank])
+        last2 = v_pass(2, HALF, last1, "last2", "after_reciprocal")
+        last3 = v_pass(3, HALF, last2, "last3", "last3")
 
         result = held.tile([P, STORIES], F32, name="result")
         v_turned = held.tile([P, HALF], F32, name="v_turned")
@@ -173,14 +171,25 @@ def tile_encodermemnn_kernel(tc, table, offs, out):
             nc.scalar.copy(v_turned[:, bank], turned[:])
         hop2 = psum.tile([P, HALF_STORIES], F32, name="hop2")
         for b in range(HALF_STORIES):
-            nc.tensor.matmul(hop2[:, b : b + 1], v_turned[:, story(b)], p_turned[:, b : b + 1], start=True, stop=True)
+            column = slice(b, b + 1)
+            nc.tensor.matmul(hop2[:, column], v_turned[:, story(b)], w_turned[:, column], start=True, stop=True)
+        for b in range(HALF_STORIES):
+            column = slice(b, b + 1)
+            nc.scalar.activation(
+                result[:, column], hop2[:, column], IDENTITY, scale=scale_spread[:, column], bias=u1[:, column]
+            )
 
         weighted = held.tile([P, BANK], F32, name="weighted")
-        nc.vector.tensor_tensor(weighted[:], last3[:, 0:BANK], p_spread[:, 0:BANK], MULT)
+        nc.vector.tensor_tensor(weighted[:], last3[:, 0:BANK], w_spread[:, 0:BANK], MULT)
         for k in range(BANK_STORIES):
             b = HALF_STORIES + k
             nc.scalar.activation(
-                unused[:], weighted[:, story(k)], IDENTITY, bias=u1_share[:, b : b + 1], accum_out=result[:, b : b + 1]
+                unused[:],
+                weighted[:, story(k)],
+                IDENTITY,
+                scale=scale_spread[:, b : b + 1],
+                bias=u1_share[:, b : b + 1],
+                accum_out=result[:, b : b + 1],
             )
         unused_product = held.tile([P, SENTENCES], F32, name="unused_product")
         for k in range(BANK_STORIES, HALF_STORIES):
@@ -189,10 +198,9 @@ def tile_encodermemnn_kernel(tc, table, offs, out):
                 unused_product[:],
                 last3[:, story(k)],
                 u1[:, b : b + 1],
-                p_spread[:, story(k)],
+                p_last[:, story(k - BANK_STORIES)],
                 ADD,
                 MULT,
                 accum_out=result[:, b : b + 1],
             )
-        nc.vector.tensor_tensor(result[:, 0:HALF_STORIES], hop2[:], u1[:, 0:HALF_STORIES], ADD)
         nc.sync.dma_start(out, result[:])

@@ -29,7 +29,6 @@ def tile_encodermemnn_kernel(tc, table, offs, out):
     nc = tc.nc
     with (
         tc.tile_pool(name="held", bufs=1) as held,
-        tc.tile_pool(name="a_passes", bufs=3) as a_passes,
         tc.psum_pool(name="psum", bufs=1) as psum,
         tc.psum_pool(name="small_psum", bufs=1) as small_psum,
     ):
@@ -49,10 +48,10 @@ def tile_encodermemnn_kernel(tc, table, offs, out):
         story_ones = held.tile([STORIES, P], F32, name="story_ones")
         nc.gpsimd.memset(story_ones[:], 1.0)
 
-        warm = held.tile([P, 1], F32, name="warm", tag="value_table")
+        warm = held.tile([P, 1], F32, name="warm")
         nc.gpsimd.memset(warm[:], 0.0)
         nc.scalar.activation(warm[:], warm[:], EXP)
-        value_table = held.tile([P, VOCAB], F32, name="value_table", tag="value_table")
+        value_table = held.tile([P, VOCAB], F32, name="value_table")
         nc.sync.dma_start(value_table[:], table[P : 2 * P, :])
 
         def story(b):
@@ -66,17 +65,26 @@ def tile_encodermemnn_kernel(tc, table, offs, out):
             else:
                 nc.vector.tensor_tensor(longer, words, shorter, ADD)
 
-        a = None
-        for t in range(WORDS):
-            longer = a_passes.tile([P, COLS], F32, name="a")
-            for first in (0, HALF):
-                half = slice(first, first + HALF)
-                add_words(address_table, t, first, None if t == 0 else a[:, half], longer[:, half])
-            a = longer
+        halves = (slice(0, HALF), slice(HALF, COLS))
+        banks = (slice(0, BANK), slice(BANK, HALF))
+        whole = (slice(0, HALF),)
+
+        def sums(window, t, first, shorter, pieces, name, tag=None):
+            longer = held.tile([P, pieces[-1].stop], F32, name=name, tag=tag or name)
+            for piece in pieces:
+                add_words(window, t, first + piece.start, None if t == 0 else shorter[:, piece], longer[:, piece])
+            return longer
+
+        a0 = sums(address_table, 0, 0, None, (slice(0, COLS),), "a0")
+        first0 = sums(value_table, 0, 0, None, whole, "first0")
+        a1 = sums(address_table, 1, 0, a0, (slice(0, COLS),), "a1")
+        first1 = sums(value_table, 1, 0, first0, whole, "first1")
+        a2 = sums(address_table, 2, 0, a1, halves, "a2")
+        a = sums(address_table, 3, 0, a2, halves, "a")
 
         u1 = held.tile([P, STORIES], F32, name="u1")
         unused = held.tile([P, SENTENCES], F32, name="unused")
-        products = held.tile([P, COLS], BF16, name="products")
+        products = held.tile([P, COLS], BF16, name="products", tag="after_maximum")
         for first in (0, HALF_STORIES):
             for b in range(first, first + HALF_STORIES):
                 nc.scalar.activation(
@@ -84,7 +92,7 @@ def tile_encodermemnn_kernel(tc, table, offs, out):
                 )
             for b in range(first, first + HALF_STORIES):
                 nc.scalar.activation(products[:, story(b)], a[:, story(b)], COPY, scale=u1[:, b : b + 1])
-        z = psum.tile([STORIES, SENTENCES], F32, name="z")
+        z = psum.tile([STORIES, SENTENCES], F32, name="z", tag="after_weights")
         for b in range(STORIES):
             nc.tensor.matmul(
                 z[:],
@@ -100,29 +108,17 @@ def tile_encodermemnn_kernel(tc, table, offs, out):
             nc.tensor.matmul(bank[:], ones[:], products[:, first : first + BANK], start=True, stop=True)
             z_spread.append(bank)
 
-        banks = (slice(0, BANK), slice(BANK, HALF))
+        first2 = sums(value_table, 2, 0, first1, whole, "first2", "a1")
+        last0 = sums(value_table, 0, HALF, None, whole, "last0")
+        first3 = sums(value_table, 3, 0, first2, whole, "first3")
 
-        def v_pass(t, first, shorter, name, tag):
-            longer = held.tile([P, HALF], F32, name=name, tag=tag)
-            for bank in banks:
-                add_words(value_table, t, first + bank.start, None if t == 0 else shorter[:, bank], longer[:, bank])
-            return longer
-
-        first0 = v_pass(0, 0, None, "first0", "first0")
-        first1 = v_pass(1, 0, first0, "first1", "first1")
-        first2 = v_pass(2, 0, first1, "first2", "first2")
-        first3 = v_pass(3, 0, first2, "first3", "first3")
-        last0 = v_pass(0, HALF, None, "last0", "first2")
-
-        z_copy = held.tile([STORIES, SENTENCES], F32, name="z_copy", tag="after_maximum")
-        nc.scalar.copy(z_copy[:], z[:])
         minus_max = held.tile([STORIES, 1], F32, name="minus_max")
-        nc.vector.reduce_max(minus_max[:], z_copy[:], axis=X, negate=True)
-        w = held.tile([STORIES, SENTENCES], F32, name="w")
-        w_sum = held.tile([STORIES, 1], F32, name="w_sum", tag="after_reciprocal")
+        nc.vector.reduce_max(minus_max[:], z[:], axis=X, negate=True)
+        w = held.tile([STORIES, SENTENCES], F32, name="w", tag="after_reciprocal")
+        w_sum = held.tile([STORIES, 1], F32, name="w_sum")
         nc.scalar.activation(w[:], z[:], EXP, bias=minus_max[:, 0:1], accum_out=w_sum[:])
 
-        w_turned_psum = small_psum.tile([P, STORIES], F32, name="small_psum")
+        w_turned_psum = psum.tile([P, STORIES], F32, name="w_turned_psum", tag="after_turn")
         nc.tensor.matmul(w_turned_psum[:], w[:], story_identity, start=True, stop=True)
         w_turned = held.tile([P, STORIES], F32, name="w_turned")
         nc.scalar.copy(w_turned[:], w_turned_psum[:])
@@ -144,7 +140,7 @@ def tile_encodermemnn_kernel(tc, table, offs, out):
                 w_spread[:, story(k)], z_spread[k // BANK_STORIES][:, story(k % BANK_STORIES)], EXP, bias=shift[:, b : b + 1]
             )
 
-        last1 = v_pass(1, HALF, last0, "last1", "after_maximum")
+        last1 = sums(value_table, 1, HALF, last0, whole, "last1", "after_maximum")
 
         w_scale = held.tile([STORIES, 1], F32, name="w_scale")
         nc.vector.reciprocal(w_scale[:], w_sum[:])
@@ -158,13 +154,13 @@ def tile_encodermemnn_kernel(tc, table, offs, out):
         u1_share = held.tile([P, STORIES], F32, name="u1_share")
         nc.scalar.activation(u1_share[:], u1[:], COPY, scale=1.0 / SENTENCES)
 
-        last2 = v_pass(2, HALF, last1, "last2", "after_reciprocal")
-        last3 = v_pass(3, HALF, last2, "last3", "last3")
+        last2 = sums(value_table, 2, HALF, last1, banks, "last2", "after_reciprocal")
+        last3 = sums(value_table, 3, HALF, last2, banks, "last3")
 
         result = held.tile([P, STORIES], F32, name="result")
         v_turned = held.tile([P, HALF], F32, name="v_turned")
-        for bank in banks:
-            turned = psum.tile([P, BANK], F32, name=f"turned{bank.start}")
+        for bank, tag in zip(banks, ("after_weights", "after_turn")):
+            turned = psum.tile([P, BANK], F32, name=f"turned{bank.start}", tag=tag)
             for k in range(BANK_STORIES):
                 b = bank.start // SENTENCES + k
                 nc.tensor.transpose(turned[:, story(k)], first3[:, story(b)], identity[:])

@@ -21,6 +21,7 @@ HALF = COLS // 2
 HALF_STORIES = STORIES // 2
 BANK = 512
 BANK_STORIES = BANK // SENTENCES
+PAIR = 2 * SENTENCES
 
 FLOPS = 2 * 2 * P * COLS
 
@@ -30,7 +31,6 @@ def tile_encodermemnn_kernel(tc, table, offs, out):
     with (
         tc.tile_pool(name="held", bufs=1) as held,
         tc.psum_pool(name="psum", bufs=1) as psum,
-        tc.psum_pool(name="small_psum", bufs=1) as small_psum,
     ):
         offsets = held.tile([P, WORDS * COLS // 16], U16, name="offsets")
         nc.sync.dma_start(offsets[:], offs)
@@ -84,7 +84,7 @@ def tile_encodermemnn_kernel(tc, table, offs, out):
 
         u1 = held.tile([P, STORIES], F32, name="u1")
         unused = held.tile([P, SENTENCES], F32, name="unused")
-        products = held.tile([P, COLS], BF16, name="products", tag="after_maximum")
+        products = held.tile([P, COLS], BF16, name="products")
         for first in (0, HALF_STORIES):
             for b in range(first, first + HALF_STORIES):
                 nc.scalar.activation(
@@ -110,10 +110,12 @@ def tile_encodermemnn_kernel(tc, table, offs, out):
 
         first2 = sums(value_table, 2, 0, first1, whole, "first2", "a1")
         last0 = sums(value_table, 0, HALF, None, whole, "last0")
-        first3 = sums(value_table, 3, 0, first2, whole, "first3")
+        first3 = [sums(value_table, 3, 0, first2, banks[:1], "first3a")]
 
         minus_max = held.tile([STORIES, 1], F32, name="minus_max")
         nc.vector.reduce_max(minus_max[:], z[:], axis=X, negate=True)
+        first3.append(sums(value_table, 3, BANK, first2[:, BANK:HALF], banks[:1], "first3b", "products"))
+
         w = held.tile([STORIES, SENTENCES], F32, name="w", tag="after_reciprocal")
         w_sum = held.tile([STORIES, 1], F32, name="w_sum")
         nc.scalar.activation(w[:], z[:], EXP, bias=minus_max[:, 0:1], accum_out=w_sum[:])
@@ -123,78 +125,97 @@ def tile_encodermemnn_kernel(tc, table, offs, out):
         w_turned = held.tile([P, STORIES], F32, name="w_turned")
         nc.scalar.copy(w_turned[:], w_turned_psum[:])
 
-        def spread(value, name):
-            diagonal = held.tile([STORIES, STORIES], F32, name=f"{name}_diagonal")
+        w_scale = held.tile([STORIES, 1], F32, name="w_scale")
+        nc.vector.reciprocal(w_scale[:], w_sum[:])
+        last1 = sums(value_table, 1, HALF, last0, whole, "last1", "after_reciprocal")
+
+        def spread(value, name, psum_tag):
+            diagonal = held.tile([STORIES, STORIES], F32, name=f"{name}_diagonal", tag=f"{name}_diagonal")
             nc.scalar.activation(diagonal[:], story_identity, COPY, scale=value[:, 0:1])
-            on_psum = small_psum.tile([P, STORIES], F32, name="small_psum")
+            on_psum = psum.tile([P, STORIES], F32, name=f"{name}_psum", tag=psum_tag)
             nc.tensor.matmul(on_psum[:], story_ones[:], diagonal[:], start=True, stop=True)
-            spread_value = held.tile([P, STORIES], F32, name=name)
+            spread_value = held.tile([P, STORIES], F32, name=name, tag=name)
             nc.scalar.copy(spread_value[:], on_psum[:])
             return spread_value
 
-        shift = spread(minus_max, "shift")
-        w_spread = held.tile([P, HALF], F32, name="w_spread")
-        for k in range(HALF_STORIES):
-            b = HALF_STORIES + k
-            nc.scalar.activation(
-                w_spread[:, story(k)], z_spread[k // BANK_STORIES][:, story(k % BANK_STORIES)], EXP, bias=shift[:, b : b + 1]
-            )
-
-        last1 = sums(value_table, 1, HALF, last0, whole, "last1", "after_maximum")
-
-        w_scale = held.tile([STORIES, 1], F32, name="w_scale")
-        nc.vector.reciprocal(w_scale[:], w_sum[:])
-        scale_spread = spread(w_scale, "scale_spread")
-        p_last = held.tile([P, BANK], F32, name="p_last")
-        for k in range(BANK_STORIES):
-            b = STORIES - BANK_STORIES + k
-            nc.scalar.activation(
-                p_last[:, story(k)], w_spread[:, story(BANK_STORIES + k)], COPY, scale=scale_spread[:, b : b + 1]
-            )
-        u1_share = held.tile([P, STORIES], F32, name="u1_share")
-        nc.scalar.activation(u1_share[:], u1[:], COPY, scale=1.0 / SENTENCES)
-
-        last2 = sums(value_table, 2, HALF, last1, banks, "last2", "after_reciprocal")
-        last3 = sums(value_table, 3, HALF, last2, banks, "last3")
+        shift = spread(minus_max, "shift", "shift_psum")
+        scale_spread = spread(w_scale, "scale_spread", "scale_psum")
 
         result = held.tile([P, STORIES], F32, name="result")
         v_turned = held.tile([P, HALF], F32, name="v_turned")
         for bank, tag in zip(banks, ("after_weights", "after_turn")):
             turned = psum.tile([P, BANK], F32, name=f"turned{bank.start}", tag=tag)
             for k in range(BANK_STORIES):
-                b = bank.start // SENTENCES + k
-                nc.tensor.transpose(turned[:, story(k)], first3[:, story(b)], identity[:])
+                nc.tensor.transpose(turned[:, story(k)], first3[bank.start // BANK][:, story(k)], identity[:])
             nc.scalar.copy(v_turned[:, bank], turned[:])
         hop2 = psum.tile([P, HALF_STORIES], F32, name="hop2")
         for b in range(HALF_STORIES):
             column = slice(b, b + 1)
             nc.tensor.matmul(hop2[:, column], v_turned[:, story(b)], w_turned[:, column], start=True, stop=True)
+        w_spread = held.tile([P, HALF], F32, name="w_spread", tag="products")
+        for k in range(HALF_STORIES):
+            b = HALF_STORIES + k
+            nc.scalar.activation(
+                w_spread[:, story(k)], z_spread[k // BANK_STORIES][:, story(k % BANK_STORIES)], EXP, bias=shift[:, b : b + 1]
+            )
+
+        p_last = held.tile([P, PAIR], F32, name="p_last")
+        for k in range(2):
+            nc.scalar.activation(
+                p_last[:, story(k)],
+                w_spread[:, story(HALF_STORIES - 2 + k)],
+                COPY,
+                scale=scale_spread[:, STORIES - 2 + k : STORIES - 1 + k],
+            )
         for b in range(HALF_STORIES):
             column = slice(b, b + 1)
             nc.scalar.activation(
                 result[:, column], hop2[:, column], IDENTITY, scale=scale_spread[:, column], bias=u1[:, column]
             )
 
-        weighted = held.tile([P, BANK], F32, name="weighted")
-        nc.vector.tensor_tensor(weighted[:], last3[:, 0:BANK], w_spread[:, 0:BANK], MULT)
-        for k in range(BANK_STORIES):
-            b = HALF_STORIES + k
-            nc.scalar.activation(
-                unused[:],
-                weighted[:, story(k)],
-                IDENTITY,
-                scale=scale_spread[:, b : b + 1],
-                bias=u1_share[:, b : b + 1],
-                accum_out=result[:, b : b + 1],
-            )
+        u1_share = held.tile([P, STORIES], F32, name="u1_share")
+        nc.scalar.activation(u1_share[:], u1[:], COPY, scale=1.0 / SENTENCES)
+
+        four, two, last_two = slice(0, BANK), slice(BANK, HALF - PAIR), slice(HALF - PAIR, HALF)
+
+        def last_words(t, shorter, longer, piece, shift_by=0):
+            within = slice(piece.start - shift_by, piece.stop - shift_by)
+            add_words(value_table, t, HALF + piece.start, shorter[:, piece], longer[:, within])
+
+        weighted = held.tile([P, HALF - PAIR], F32, name="weighted")
+
+        def weigh_and_sum(v, columns, piece):
+            nc.vector.tensor_tensor(weighted[:, piece], v[:, columns], w_spread[:, piece], MULT)
+            for k in range(piece.start // SENTENCES, piece.stop // SENTENCES):
+                b = HALF_STORIES + k
+                nc.scalar.activation(
+                    unused[:],
+                    weighted[:, story(k)],
+                    IDENTITY,
+                    scale=scale_spread[:, b : b + 1],
+                    bias=u1_share[:, b : b + 1],
+                    accum_out=result[:, b : b + 1],
+                )
+
+        last2 = held.tile([P, HALF], F32, name="last2", tag="scale_spread_diagonal")
+        last_words(2, last1, last2, four)
+        last_words(2, last1, last2, two)
+        last3_four = held.tile([P, BANK], F32, name="last3_four")
+        last_words(3, last2, last3_four, four)
+        last_words(2, last1, last2, last_two)
+        weigh_and_sum(last3_four, four, four)
+        last3_rest = held.tile([P, BANK], F32, name="last3_rest", tag="shift")
+        last_words(3, last2, last3_rest, two, BANK)
+        last_words(3, last2, last3_rest, last_two, BANK)
+        weigh_and_sum(last3_rest, slice(0, PAIR), two)
         unused_product = held.tile([P, SENTENCES], F32, name="unused_product")
-        for k in range(BANK_STORIES, HALF_STORIES):
-            b = HALF_STORIES + k
+        for k in range(2):
+            b = STORIES - 2 + k
             nc.vector.scalar_tensor_tensor(
                 unused_product[:],
-                last3[:, story(k)],
+                last3_rest[:, story(2 + k)],
                 u1[:, b : b + 1],
-                p_last[:, story(k - BANK_STORIES)],
+                p_last[:, story(k)],
                 ADD,
                 MULT,
                 accum_out=result[:, b : b + 1],

@@ -83,12 +83,12 @@ def tile_encodermemnn_kernel(tc, table, offs, out):
         a = sums(address_table, 3, 0, a2, halves, "a")
 
         u1 = held.tile([P, STORIES], F32, name="u1")
-        unused = held.tile([P, SENTENCES], F32, name="unused")
+        unused = held.tile([P, COLS], F32, name="unused")
         products = held.tile([P, COLS], BF16, name="products")
         for first in (0, HALF_STORIES):
             for b in range(first, first + HALF_STORIES):
                 nc.scalar.activation(
-                    unused[:], a[:, story(b)], COPY, scale=1.0 / SENTENCES, accum_out=u1[:, b : b + 1]
+                    unused[:, story(b)], a[:, story(b)], COPY, scale=1.0 / SENTENCES, accum_out=u1[:, b : b + 1]
                 )
             for b in range(first, first + HALF_STORIES):
                 nc.scalar.activation(products[:, story(b)], a[:, story(b)], COPY, scale=u1[:, b : b + 1])
@@ -183,13 +183,14 @@ def tile_encodermemnn_kernel(tc, table, offs, out):
             add_words(value_table, t, HALF + piece.start, shorter[:, piece], longer[:, within])
 
         weighted = held.tile([P, HALF - PAIR], F32, name="weighted")
+        unused_sums = held.tile([P, HALF - PAIR], F32, name="unused_sums")
 
         def weigh_and_sum(v, columns, piece):
             nc.vector.tensor_tensor(weighted[:, piece], v[:, columns], w_spread[:, piece], MULT)
             for k in range(piece.start // SENTENCES, piece.stop // SENTENCES):
                 b = HALF_STORIES + k
                 nc.scalar.activation(
-                    unused[:],
+                    unused_sums[:, story(k)],
                     weighted[:, story(k)],
                     IDENTITY,
                     scale=scale_spread[:, b : b + 1],
@@ -208,11 +209,11 @@ def tile_encodermemnn_kernel(tc, table, offs, out):
         last_words(3, last2, last3_rest, two, BANK)
         last_words(3, last2, last3_rest, last_two, BANK)
         weigh_and_sum(last3_rest, slice(0, PAIR), two)
-        unused_product = held.tile([P, SENTENCES], F32, name="unused_product")
+        unused_product = held.tile([P, PAIR], F32, name="unused_product")
         for k in range(2):
             b = STORIES - 2 + k
             nc.vector.scalar_tensor_tensor(
-                unused_product[:],
+                unused_product[:, story(k)],
                 last3_rest[:, story(2 + k)],
                 u1[:, b : b + 1],
                 p_last[:, story(k)],

@@ -127,7 +127,7 @@ def tile_encodermemnn_kernel(tc, table, offs, out):
 
         w_scale = held.tile([STORIES, 1], F32, name="w_scale")
         nc.vector.reciprocal(w_scale[:], w_sum[:])
-        last1 = sums(value_table, 1, HALF, last0, whole, "last1", "after_reciprocal")
+        last1 = sums(value_table, 1, HALF, last0, banks, "last1", "after_reciprocal")
 
         def spread(value, name, psum_tag):
             diagonal = held.tile([STORIES, STORIES], F32, name=f"{name}_diagonal", tag=f"{name}_diagonal")
@@ -161,11 +161,9 @@ def tile_encodermemnn_kernel(tc, table, offs, out):
 
         p_last = held.tile([P, PAIR], F32, name="p_last")
         for k in range(2):
+            b = STORIES - 2 + k
             nc.scalar.activation(
-                p_last[:, story(k)],
-                w_spread[:, story(HALF_STORIES - 2 + k)],
-                COPY,
-                scale=scale_spread[:, STORIES - 2 + k : STORIES - 1 + k],
+                p_last[:, story(k)], w_spread[:, story(HALF_STORIES - 2 + k)], COPY, scale=scale_spread[:, b : b + 1]
             )
         for b in range(HALF_STORIES):
             column = slice(b, b + 1)
@@ -176,17 +174,18 @@ def tile_encodermemnn_kernel(tc, table, offs, out):
         u1_share = held.tile([P, STORIES], F32, name="u1_share")
         nc.scalar.activation(u1_share[:], u1[:], COPY, scale=1.0 / SENTENCES)
 
-        four, two, last_two = slice(0, BANK), slice(BANK, HALF - PAIR), slice(HALF - PAIR, HALF)
+        last2 = sums(value_table, 2, HALF, last1, banks, "last2", "scale_spread_diagonal")
 
-        def last_words(t, shorter, longer, piece, shift_by=0):
-            within = slice(piece.start - shift_by, piece.stop - shift_by)
-            add_words(value_table, t, HALF + piece.start, shorter[:, piece], longer[:, within])
+        def fourth_words(piece, name, tag):
+            longer = held.tile([P, piece.stop - piece.start], F32, name=name, tag=tag)
+            add_words(value_table, 3, HALF + piece.start, last2[:, piece], longer[:])
+            return longer
 
         weighted = held.tile([P, HALF - PAIR], F32, name="weighted")
         unused_sums = held.tile([P, HALF - PAIR], F32, name="unused_sums")
 
-        def weigh_and_sum(v, columns, piece):
-            nc.vector.tensor_tensor(weighted[:, piece], v[:, columns], w_spread[:, piece], MULT)
+        def weigh_and_sum(v, piece):
+            nc.vector.tensor_tensor(weighted[:, piece], v, w_spread[:, piece], MULT)
             for k in range(piece.start // SENTENCES, piece.stop // SENTENCES):
                 b = HALF_STORIES + k
                 nc.scalar.activation(
@@ -198,27 +197,25 @@ def tile_encodermemnn_kernel(tc, table, offs, out):
                     accum_out=result[:, b : b + 1],
                 )
 
-        last2 = held.tile([P, HALF], F32, name="last2", tag="scale_spread_diagonal")
-        last_words(2, last1, last2, four)
-        last_words(2, last1, last2, two)
-        last3_four = held.tile([P, BANK], F32, name="last3_four")
-        last_words(3, last2, last3_four, four)
-        last_words(2, last1, last2, last_two)
-        weigh_and_sum(last3_four, four, four)
-        last3_rest = held.tile([P, BANK], F32, name="last3_rest", tag="shift")
-        last_words(3, last2, last3_rest, two, BANK)
-        last_words(3, last2, last3_rest, last_two, BANK)
-        weigh_and_sum(last3_rest, slice(0, PAIR), two)
-        unused_product = held.tile([P, PAIR], F32, name="unused_product")
-        for k in range(2):
+        unused_products = held.tile([P, PAIR], F32, name="unused_products")
+
+        def weigh_with_sum(v, k):
             b = STORIES - 2 + k
             nc.vector.scalar_tensor_tensor(
-                unused_product[:, story(k)],
-                last3_rest[:, story(2 + k)],
+                unused_products[:, story(k)],
+                v,
                 u1[:, b : b + 1],
                 p_last[:, story(k)],
                 ADD,
                 MULT,
                 accum_out=result[:, b : b + 1],
             )
+
+        last3_four = fourth_words(slice(0, BANK), "last3_four", "last3_four")
+        last3_three = fourth_words(slice(BANK, HALF - SENTENCES), "last3_three", "last3_three")
+        weigh_and_sum(last3_four[:], slice(0, BANK))
+        weigh_and_sum(last3_three[:, 0:PAIR], slice(BANK, HALF - PAIR))
+        last3_one = fourth_words(slice(HALF - SENTENCES, HALF), "last3_one", "shift")
+        weigh_with_sum(last3_three[:, story(2)], 0)
+        weigh_with_sum(last3_one[:], 1)
         nc.sync.dma_start(out, result[:])

@@ -211,11 +211,12 @@ def tile_encodermemnn_kernel(tc, table, offs, out):
                 accum_out=result[:, b : b + 1],
             )
 
-        last3_four = fourth_words(slice(0, BANK), "last3_four", "last3_four")
-        last3_three = fourth_words(slice(BANK, HALF - SENTENCES), "last3_three", "last3_three")
-        weigh_and_sum(last3_four[:], slice(0, BANK))
-        weigh_and_sum(last3_three[:, 0:PAIR], slice(BANK, HALF - PAIR))
-        last3_one = fourth_words(slice(HALF - SENTENCES, HALF), "last3_one", "shift")
-        weigh_with_sum(last3_three[:, story(2)], 0)
-        weigh_with_sum(last3_one[:], 1)
+        four, two, last_two = slice(0, BANK), slice(BANK, HALF - PAIR), slice(HALF - PAIR, HALF)
+        last3_four = fourth_words(four, "last3_four", "last3_four")
+        last3_two = fourth_words(two, "last3_two", "last3_two")
+        weigh_and_sum(last3_four[:], four)
+        last3_last_two = fourth_words(last_two, "last3_last_two", "shift")
+        weigh_and_sum(last3_two[:], two)
+        for k in range(2):
+            weigh_with_sum(last3_last_two[:, story(k)], k)
         nc.sync.dma_start(out, result[:])

@@ -68,6 +68,7 @@ def tile_encodermemnn_kernel(tc, table, offs, out):
         halves = (slice(0, HALF), slice(HALF, COLS))
         banks = (slice(0, BANK), slice(BANK, HALF))
         whole = (slice(0, HALF),)
+        last_a_pieces = tuple(slice(b * SENTENCES, e * SENTENCES) for b, e in ((0, 4), (4, 10), (10, 16)))
 
         def sums(window, t, first, shorter, pieces, name, tag=None):
             longer = held.tile([P, pieces[-1].stop], F32, name=name, tag=tag or name)
@@ -80,17 +81,18 @@ def tile_encodermemnn_kernel(tc, table, offs, out):
         a1 = sums(address_table, 1, 0, a0, (slice(0, COLS),), "a1")
         first1 = sums(value_table, 1, 0, first0, whole, "first1")
         a2 = sums(address_table, 2, 0, a1, halves, "a2")
-        a = sums(address_table, 3, 0, a2, halves, "a")
+        a = sums(address_table, 3, 0, a2, last_a_pieces, "a")
 
         u1 = held.tile([P, STORIES], F32, name="u1")
         unused = held.tile([P, COLS], F32, name="unused")
         products = held.tile([P, COLS], BF16, name="products")
-        for first in (0, HALF_STORIES):
-            for b in range(first, first + HALF_STORIES):
+        for piece in last_a_pieces:
+            stories = range(piece.start // SENTENCES, piece.stop // SENTENCES)
+            for b in stories:
                 nc.scalar.activation(
                     unused[:, story(b)], a[:, story(b)], COPY, scale=1.0 / SENTENCES, accum_out=u1[:, b : b + 1]
                 )
-            for b in range(first, first + HALF_STORIES):
+            for b in stories:
                 nc.scalar.activation(products[:, story(b)], a[:, story(b)], COPY, scale=u1[:, b : b + 1])
         z = psum.tile([STORIES, SENTENCES], F32, name="z", tag="after_weights")
         for b in range(STORIES):
@@ -110,11 +112,13 @@ def tile_encodermemnn_kernel(tc, table, offs, out):
 
         first2 = sums(value_table, 2, 0, first1, whole, "first2", "a1")
         last0 = sums(value_table, 0, HALF, None, whole, "last0")
-        first3 = [sums(value_table, 3, 0, first2, banks[:1], "first3a")]
 
         minus_max = held.tile([STORIES, 1], F32, name="minus_max")
         nc.vector.reduce_max(minus_max[:], z[:], axis=X, negate=True)
-        first3.append(sums(value_table, 3, BANK, first2[:, BANK:HALF], banks[:1], "first3b", "products"))
+        first3 = [
+            sums(value_table, 3, 0, first2, banks[:1], "first3a", "products"),
+            sums(value_table, 3, BANK, first2[:, BANK:HALF], banks[:1], "first3b", "ones"),
+        ]
 
         w = held.tile([STORIES, SENTENCES], F32, name="w", tag="after_reciprocal")
         w_sum = held.tile([STORIES, 1], F32, name="w_sum")
@@ -152,7 +156,7 @@ def tile_encodermemnn_kernel(tc, table, offs, out):
         for b in range(HALF_STORIES):
             column = slice(b, b + 1)
             nc.tensor.matmul(hop2[:, column], v_turned[:, story(b)], w_turned[:, column], start=True, stop=True)
-        w_spread = held.tile([P, HALF], F32, name="w_spread", tag="products")
+        w_spread = held.tile([P, HALF], F32, name="w_spread", tag="ones")
         for k in range(HALF_STORIES):
             b = HALF_STORIES + k
             nc.scalar.activation(

import concourse.mybir as mybir
from concourse.masks import make_identity

F32 = mybir.dt.float32
BF16 = mybir.dt.bfloat16
U16 = mybir.dt.uint16
ADD = mybir.AluOpType.add
MULT = mybir.AluOpType.mult
COPY = mybir.ActivationFunctionType.Copy
IDENTITY = mybir.ActivationFunctionType.Identity
EXP = mybir.ActivationFunctionType.Exp
X = mybir.AxisListType.X

P = 128
VOCAB = 2048
STORIES = 16
SENTENCES = 128
WORDS = 4
COLS = STORIES * SENTENCES
HALF = COLS // 2
HALF_STORIES = STORIES // 2
BANK = 512
BANK_STORIES = BANK // SENTENCES
PAIR = 2 * SENTENCES

FLOPS = 2 * 2 * P * COLS


def tile_encodermemnn_kernel(tc, table, offs, out):
    nc = tc.nc
    with (
        tc.tile_pool(name="held", bufs=1) as held,
        tc.psum_pool(name="psum", bufs=1) as psum,
    ):
        offsets = held.tile([P, WORDS * COLS // 16], U16, name="offsets")
        nc.sync.dma_start(offsets[:], offs)
        address_table = held.tile([P, VOCAB], F32, name="address_table")
        nc.sync.dma_start(address_table[:], table[0:P, :])

        identity = held.tile([P, P], F32, name="identity")
        make_identity(nc, identity[:])
        story_identity = identity[0:STORIES, 0:STORIES]
        selector = held.tile([P, 2 * STORIES - 1], BF16, name="selector")
        nc.gpsimd.memset(selector[:], 0.0)
        nc.gpsimd.memset(selector[:, STORIES - 1 : STORIES], 1.0)
        ones = held.tile([P, P], BF16, name="ones")
        nc.gpsimd.memset(ones[:], 1.0)
        story_ones = held.tile([STORIES, P], F32, name="story_ones")
        nc.gpsimd.memset(story_ones[:], 1.0)

        warm = held.tile([P, 1], F32, name="warm")
        nc.gpsimd.memset(warm[:], 0.0)
        nc.scalar.activation(warm[:], warm[:], EXP)
        value_table = held.tile([P, VOCAB], F32, name="value_table")
        nc.sync.dma_start(value_table[:], table[P : 2 * P, :])

        def story(b):
            return slice(b * SENTENCES, (b + 1) * SENTENCES)

        def add_words(window, t, first, shorter, longer):
            entry = t * COLS + first
            words = window[:].indirect(offsets[:, entry // 16 : (entry + longer.shape[1]) // 16])
            if t == 0:
                nc.vector.tensor_copy(longer, words)
            else:
                nc.vector.tensor_tensor(longer, words, shorter, ADD)

        halves = (slice(0, HALF), slice(HALF, COLS))
        banks = (slice(0, BANK), slice(BANK, HALF))
        whole = (slice(0, HALF),)
        last_a_pieces = tuple(slice(b * SENTENCES, e * SENTENCES) for b, e in ((0, 4), (4, 10), (10, 16)))

        def sums(window, t, first, shorter, pieces, name, tag=None):
            longer = held.tile([P, pieces[-1].stop], F32, name=name, tag=tag or name)
            for piece in pieces:
                add_words(window, t, first + piece.start, None if t == 0 else shorter[:, piece], longer[:, piece])
            return longer

        a0 = sums(address_table, 0, 0, None, (slice(0, COLS),), "a0")
        first0 = sums(value_table, 0, 0, None, whole, "first0")
        a1 = sums(address_table, 1, 0, a0, (slice(0, COLS),), "a1")
        first1 = sums(value_table, 1, 0, first0, whole, "first1")
        a2 = sums(address_table, 2, 0, a1, halves, "a2")
        a = sums(address_table, 3, 0, a2, last_a_pieces, "a")

        u1 = held.tile([P, STORIES], F32, name="u1")
        unused = held.tile([P, COLS], F32, name="unused")
        products = held.tile([P, COLS], BF16, name="products")
        for piece in last_a_pieces:
            stories = range(piece.start // SENTENCES, piece.stop // SENTENCES)
            for b in stories:
                nc.scalar.activation(
                    unused[:, story(b)], a[:, story(b)], COPY, scale=1.0 / SENTENCES, accum_out=u1[:, b : b + 1]
                )
            for b in stories:
                nc.scalar.activation(products[:, story(b)], a[:, story(b)], COPY, scale=u1[:, b : b + 1])
        z = psum.tile([STORIES, SENTENCES], F32, name="z", tag="after_weights")
        for b in range(STORIES):
            nc.tensor.matmul(
                z[:],
                selector[:, STORIES - 1 - b : 2 * STORIES - 1 - b],
                products[:, story(b)],
                start=(b == 0),
                stop=(b == STORIES - 1),
            )

        z_spread = []
        for first in range(HALF, COLS, BANK):
            bank = psum.tile([P, BANK], F32, name=f"z_spread{first}")
            nc.tensor.matmul(bank[:], ones[:], products[:, first : first + BANK], start=True, stop=True)
            z_spread.append(bank)

        first2 = sums(value_table, 2, 0, first1, whole, "first2", "a1")
        last0 = sums(value_table, 0, HALF, None, whole, "last0")

        minus_max = held.tile([STORIES, 1], F32, name="minus_max")
        nc.vector.reduce_max(minus_max[:], z[:], axis=X, negate=True)
        first3 = [
            sums(value_table, 3, 0, first2, banks[:1], "first3a", "products"),
            sums(value_table, 3, BANK, first2[:, BANK:HALF], banks[:1], "first3b", "ones"),
        ]

        w = held.tile([STORIES, SENTENCES], F32, name="w", tag="after_reciprocal")
        w_sum = held.tile([STORIES, 1], F32, name="w_sum")
        nc.scalar.activation(w[:], z[:], EXP, bias=minus_max[:, 0:1], accum_out=w_sum[:])

        w_turned_psum = psum.tile([P, STORIES], F32, name="w_turned_psum", tag="after_turn")
        nc.tensor.matmul(w_turned_psum[:], w[:], story_identity, start=True, stop=True)
        w_turned = held.tile([P, STORIES], F32, name="w_turned")
        nc.scalar.copy(w_turned[:], w_turned_psum[:])

        w_scale = held.tile([STORIES, 1], F32, name="w_scale")
        nc.vector.reciprocal(w_scale[:], w_sum[:])
        last1 = sums(value_table, 1, HALF, last0, banks, "last1", "after_reciprocal")

        def spread(value, name, psum_tag):
            diagonal = held.tile([STORIES, STORIES], F32, name=f"{name}_diagonal", tag=f"{name}_diagonal")
            nc.scalar.activation(diagonal[:], story_identity, COPY, scale=value[:, 0:1])
            on_psum = psum.tile([P, STORIES], F32, name=f"{name}_psum", tag=psum_tag)
            nc.tensor.matmul(on_psum[:], story_ones[:], diagonal[:], start=True, stop=True)
            spread_value = held.tile([P, STORIES], F32, name=name, tag=name)
            nc.scalar.copy(spread_value[:], on_psum[:])
            return spread_value

        shift = spread(minus_max, "shift", "shift_psum")
        scale_spread = spread(w_scale, "scale_spread", "scale_psum")

        result = held.tile([P, STORIES], F32, name="result")
        v_turned = held.tile([P, HALF], F32, name="v_turned")
        for bank, tag in zip(banks, ("after_weights", "after_turn")):
            turned = psum.tile([P, BANK], F32, name=f"turned{bank.start}", tag=tag)
            for k in range(BANK_STORIES):
                nc.tensor.transpose(turned[:, story(k)], first3[bank.start // BANK][:, story(k)], identity[:])
            nc.scalar.copy(v_turned[:, bank], turned[:])
        hop2 = psum.tile([P, HALF_STORIES], F32, name="hop2")
        for b in range(HALF_STORIES):
            column = slice(b, b + 1)
            nc.tensor.matmul(hop2[:, column], v_turned[:, story(b)], w_turned[:, column], start=True, stop=True)
        w_spread = held.tile([P, HALF], F32, name="w_spread", tag="ones")
        for k in range(HALF_STORIES):
            b = HALF_STORIES + k
            nc.scalar.activation(
                w_spread[:, story(k)], z_spread[k // BANK_STORIES][:, story(k % BANK_STORIES)], EXP, bias=shift[:, b : b + 1]
            )

        p_last = held.tile([P, PAIR], F32, name="p_last")
        for k in range(2):
            b = STORIES - 2 + k
            nc.scalar.activation(
                p_last[:, story(k)], w_spread[:, story(HALF_STORIES - 2 + k)], COPY, scale=scale_spread[:, b : b + 1]
            )
        for b in range(HALF_STORIES):
            column = slice(b, b + 1)
            nc.scalar.activation(
                result[:, column], hop2[:, column], IDENTITY, scale=scale_spread[:, column], bias=u1[:, column]
            )

        u1_share = held.tile([P, STORIES], F32, name="u1_share")
        nc.scalar.activation(u1_share[:], u1[:], COPY, scale=1.0 / SENTENCES)

        last2 = sums(value_table, 2, HALF, last1, banks, "last2", "scale_spread_diagonal")

        def fourth_words(piece, name, tag):
            longer = held.tile([P, piece.stop - piece.start], F32, name=name, tag=tag)
            add_words(value_table, 3, HALF + piece.start, last2[:, piece], longer[:])
            return longer

        weighted = held.tile([P, HALF - PAIR], F32, name="weighted")
        unused_sums = held.tile([P, HALF - PAIR], F32, name="unused_sums")

        def weigh_and_sum(v, piece):
            nc.vector.tensor_tensor(weighted[:, piece], v, w_spread[:, piece], MULT)
            for k in range(piece.start // SENTENCES, piece.stop // SENTENCES):
                b = HALF_STORIES + k
                nc.scalar.activation(
                    unused_sums[:, story(k)],
                    weighted[:, story(k)],
                    IDENTITY,
                    scale=scale_spread[:, b : b + 1],
                    bias=u1_share[:, b : b + 1],
                    accum_out=result[:, b : b + 1],
                )

        unused_products = held.tile([P, PAIR], F32, name="unused_products")

        def weigh_with_sum(v, k):
            b = STORIES - 2 + k
            nc.vector.scalar_tensor_tensor(
                unused_products[:, story(k)],
                v,
                u1[:, b : b + 1],
                p_last[:, story(k)],
                ADD,
                MULT,
                accum_out=result[:, b : b + 1],
            )

        four, two, last_two = slice(0, BANK), slice(BANK, HALF - PAIR), slice(HALF - PAIR, HALF)
        last3_four = fourth_words(four, "last3_four", "last3_four")
        last3_two = fourth_words(two, "last3_two", "last3_two")
        weigh_and_sum(last3_four[:], four)
        last3_last_two = fourth_words(last_two, "last3_last_two", "shift")
        weigh_and_sum(last3_two[:], two)
        for k in range(2):
            weigh_with_sum(last3_last_two[:, story(k)], k)
        nc.sync.dma_start(out, result[:])
